import numpy as np
import ml_dtypes


def mxq(x, axis, fmt="e4m3"):
    dtype, down = {"e4m3": (ml_dtypes.float8_e4m3fn, 7), "e5m2": (ml_dtypes.float8_e5m2, 14)}[fmt]
    v = np.moveaxis(np.asarray(x, np.float32).astype(ml_dtypes.bfloat16).astype(np.float64), axis, -1)
    blocks = v.reshape(v.shape[:-1] + (-1, 32))
    amax = np.abs(blocks).max(-1, keepdims=True)
    byte = np.maximum(np.where(amax > 0, np.frexp(amax)[1] - 1 + 127, 0) - down, 1)
    scale = np.exp2(byte - 127.0)
    codes = (blocks / scale).astype(np.float32).astype(dtype).astype(np.float64)
    return np.moveaxis((codes * scale).reshape(v.shape), -1, axis)


WIDE = False


def mx_kscale(k):
    if not WIDE:
        return np.ones(k)
    levels = np.array([10, -10, 5, -5, 0])
    if k % 512:
        return np.exp2(np.random.permutation(np.resize(levels, k // 32))).repeat(32)
    a = np.empty((k // 512, 16))
    for p in range(k // 512):
        a[p, :8] = np.random.permutation(np.resize(levels, 8))
        for g in range(8):
            far = levels[np.abs(levels - a[p, g]) >= 10]
            a[p, g + 8] = far[np.random.randint(len(far))]
    return np.exp2(a.ravel()).repeat(32)


BF16 = ml_dtypes.bfloat16


def bf(x):
    return np.asarray(x, np.float32).astype(BF16)


def f64(x):
    return np.asarray(x).astype(np.float64)


N, D, H, HD = 4096, 512, 8, 64
P = H * HD
HALF = HD // 2
EPS = 1e-6


def rms_norm(y):
    ms = np.mean(y * y, axis=-1, keepdims=True) + EPS
    return y * (1.0 / np.sqrt(ms))


def rotate_half(z):
    h = z.shape[-1] // 2
    return np.concatenate([-z[..., h:], z[..., :h]], axis=-1)


def rope_2d(y, cos, sin):
    def ap(z, c, s):
        return z * c[:, None, :] + rotate_half(z) * s[:, None, :]

    return np.concatenate([ap(y[..., :HALF], cos[:, :HALF], sin[:, :HALF]), ap(y[..., HALF:], cos[:, HALF:], sin[:, HALF:])], axis=-1)


def setup_inputs():
    s = mx_kscale(D)
    return {
        "hidden_states": bf(np.random.standard_normal((N, D)) * s),
        "cos": bf(np.random.uniform(-1.0, 1.0, (N, HD))),
        "sin": bf(np.random.uniform(-1.0, 1.0, (N, HD))),
        "Wq": bf(np.random.standard_normal((D, P)) / np.sqrt(D) / s[:, None]),
        "Wk": bf(np.random.standard_normal((D, P)) / np.sqrt(D) / s[:, None]),
        "Wv": bf(np.random.standard_normal((D, P)) / np.sqrt(D) / s[:, None]),
        "q_scale": bf(1.0 + 0.1 * np.random.standard_normal(HD)),
        "k_scale": bf(1.0 + 0.1 * np.random.standard_normal(HD)),
    }


def reference(hidden_states, cos, sin, Wq, Wk, Wv, q_scale, k_scale):
    x = mxq(f64(hidden_states), 1, "e4m3")
    c, s = f64(cos), f64(sin)
    yq = (x @ mxq(f64(Wq), 0, "e4m3")).reshape(N, H, HD)
    yk = (x @ mxq(f64(Wk), 0, "e4m3")).reshape(N, H, HD)
    yv = (x @ mxq(f64(Wv), 0, "e4m3")).reshape(N, H, HD)
    q = rms_norm(yq) * f64(q_scale)
    k = rms_norm(yk) * f64(k_scale)
    v = rms_norm(yv)
    return rope_2d(q, c, s), rope_2d(k, c, s), v

@@ -1,0 +1,261 @@
+from contextlib import ExitStack
+
+import concourse.mybir as mybir
+from concourse.masks import make_identity
+
+F32 = mybir.dt.float32
+BF16 = mybir.dt.bfloat16
+U32 = mybir.dt.uint32
+U8 = mybir.dt.uint8
+FP8X4 = mybir.dt.float8_e4m3fn_x4
+ALU = mybir.AluOpType
+ACT = mybir.ActivationFunctionType
+
+N, D, H, HD = 4096, 512, 8, 64
+P = 128
+PACK = 4
+NT = N // P
+NPAIR = NT // 2
+TAB = 4
+NTAB = NT // TAB
+LAG = 4
+RING = 7
+EPS = 1e-6
+FLOPS = 2 * N * D * 3 * H * HD
+
+
+def tile_torchgemma4visionattention_pa_t_kernel(
+    tc, hidden_states, cos, sin, Wq, Wk, Wv, q_scale, k_scale, out_0, out_1, out_2
+):
+    nc = tc.nc
+    with ExitStack() as ctx:
+        ctx.enter_context(tc.manual_schedule())
+        const = ctx.enter_context(tc.tile_pool(name="const", bufs=1))
+        x_in = ctx.enter_context(tc.tile_pool(name="x_in", bufs=NPAIR))
+        x_grouped = ctx.enter_context(tc.tile_pool(name="x_grouped", bufs=2))
+        x_mx = ctx.enter_context(tc.tile_pool(name="x_mx", bufs=4))
+        small = ctx.enter_context(tc.tile_pool(name="small", bufs=4))
+        work = ctx.enter_context(tc.tile_pool(name="work", bufs=4))
+        psum_t = ctx.enter_context(tc.psum_pool(name="psum_t", bufs=1))
+        psum_y = ctx.enter_context(tc.psum_pool(name="psum_y", bufs=RING))
+
+        x_view = hidden_states.rearrange("(p t) d -> p t d", t=NT)
+        cos_view = cos.rearrange("(p t) f -> p t f", t=NT)
+        sin_view = sin.rearrange("(p t) f -> p t f", t=NT)
+        out_views = [o.rearrange("(p t) h f -> p t (h f)", t=NT) for o in (out_0, out_1, out_2)]
+
+        w_raw = []
+        x_raw = []
+
+        def load_w(w, label):
+            raw = const.tile([P, PACK, D], BF16, name="w_raw_" + label)
+            nc.sync.dma_start(out=raw[:], in_=w.rearrange("(p j) c -> p j c", j=PACK))
+            w_raw.append(raw)
+
+        def load_x(pair):
+            raw = x_in.tile([P, 2, D], BF16, name="x_raw")
+            nc.sync.dma_start(out=raw[:], in_=x_view[:, 2 * pair : 2 * pair + 2, :])
+            x_raw.append(raw)
+
+        gains = const.tile([P, 2, HD], BF16, name="gains")
+        cos_sb = const.tile([P, NT, HD], BF16, name="cos_sb")
+        sin_sb = const.tile([P, NT, HD], BF16, name="sin_sb")
+        load_x(0)
+        load_w(Wq, "q")
+        load_w(Wk, "k")
+        load_w(Wv, "v")
+        nc.sync.dma_start(out=gains[:, 0, :], in_=q_scale.partition_broadcast(P))
+        nc.sync.dma_start(out=gains[:, 1, :], in_=k_scale.partition_broadcast(P))
+        nc.sync.dma_start(out=cos_sb[:, 0:TAB, :], in_=cos_view[:, 0:TAB, :])
+        nc.sync.dma_start(out=sin_sb[:, 0:TAB, :], in_=sin_view[:, 0:TAB, :])
+        load_x(1)
+        nc.sync.dma_start(out=sin_sb[:, TAB:NT, :], in_=sin_view[:, TAB:NT, :])
+        nc.sync.dma_start(out=cos_sb[:, TAB:NT, :], in_=cos_view[:, TAB:NT, :])
+        for pair in range(2, NPAIR):
+            load_x(pair)
+
+        identity = const.tile([P, P], F32, name="identity")
+        make_identity(nc, identity[:])
+        eps_tile = const.tile([P, 1], F32, name="eps_tile")
+        nc.vector.memset(eps_tile[:], EPS)
+        warm = const.tile([P, 1], F32, name="warm")
+        nc.scalar.activation(out=warm[:], in_=eps_tile[:], func=ACT.Abs_reciprocal_sqrt)
+
+        w_codes = const.tile([P, 3 * D], U32, name="w_codes", align_bytes=64)
+        w_scales = const.tile([P, 3 * D], U8, name="w_scales", align_bytes=64)
+        w_grouped = [const.tile([P, D, PACK], BF16, name="w_grouped%d" % i, align_bytes=64) for i in range(3)]
+
+        def regroup_w(i, copy):
+            copy(
+                out=w_grouped[i][:].rearrange("p (c i) t -> p c t i", i=4),
+                in_=w_raw[i][:].rearrange("p t (c i) -> p c t i", i=4),
+            )
+
+        def quantise_w(i):
+            nc.vector.quantize_mx(
+                out=w_codes[:, i * D : (i + 1) * D].bitcast(FP8X4),
+                scales=w_scales[:, i * D : (i + 1) * D],
+                in_=w_grouped[i][:].rearrange("p c t -> p (c t)"),
+            )
+
+        sin_swapped = const.tile([P, NT, HD], BF16, name="sin_swapped")
+        table = const.tile([P, NT, 2, 2, HD], F32, name="table")
+
+        def swap_sin(t0, t1):
+            plain = sin_sb[:, t0:t1, :].rearrange("p t (b s i) -> p (t b) s i", b=2, s=2)
+            swapped = sin_swapped[:, t0:t1, :].rearrange("p t (b s i) -> p (t b) s i", b=2, s=2)
+            nc.vector.tensor_copy(out=swapped[:, :, 0, :], in_=plain[:, :, 1, :])
+            nc.vector.tensor_scalar(
+                out=swapped[:, :, 1, :], in0=plain[:, :, 0, :], scalar1=-1.0, scalar2=None, op0=ALU.mult
+            )
+
+        def build_table(chunk, product):
+            tiles = slice(chunk * TAB, (chunk + 1) * TAB)
+            angle = cos_sb if product == 0 else sin_swapped
+            nc.gpsimd.tensor_tensor(
+                out=table[:, tiles, :, product, :],
+                in0=angle[:, tiles, :].unsqueeze(2).to_broadcast([P, TAB, 2, HD]),
+                in1=gains[:].unsqueeze(1).to_broadcast([P, TAB, 2, HD]),
+                op=ALU.mult,
+            )
+
+        x_banks = {}
+        x_groups = {}
+        x_codes = {}
+
+        def transpose_x(pair):
+            words = x_raw[pair][:].bitcast(F32)
+            bank = psum_t.tile([P, 2, 2, P], F32, name="x_bank")
+            for a in range(2):
+                for u in range(2):
+                    nc.tensor.transpose(bank[:, a, u, :], words[:, a, u : 2 * P : 2], identity[:])
+            x_banks[pair] = bank
+
+        def copy_x(pair, copy):
+            grouped = x_grouped.tile([P, 2, P, PACK], BF16, name="x_group", align_bytes=64)
+            as_words = grouped[:].rearrange("p a n t -> p a (n t)").bitcast(F32).rearrange("p a (n u) -> p a n u", u=2)
+            copy(out=as_words, in_=x_banks[pair][:].rearrange("p a u n -> p a n u"))
+            x_groups[pair] = grouped
+
+        def quantise_x(pair):
+            codes = x_mx.tile([P, 2 * P], U32, name="x_code", align_bytes=64)
+            scales = x_mx.tile([P, 2 * P], U8, name="x_scale", align_bytes=64)
+            nc.vector.quantize_mx(
+                out=codes[:].bitcast(FP8X4), scales=scales[:], in_=x_groups[pair][:].rearrange("p a n t -> p (a n t)")
+            )
+            x_codes[pair] = (codes, scales)
+
+        def x_copier(pair):
+            return nc.scalar.copy if pair % 2 == 0 else nc.vector.tensor_copy
+
+        pair_behind_tile = {max(2 * pair - 3, 0): pair for pair in range(1, NPAIR)}
+
+        transpose_x(0)
+        copy_x(0, x_copier(0))
+        regroup_w(0, nc.vector.tensor_copy)
+        regroup_w(1, nc.scalar.copy)
+        quantise_x(0)
+        quantise_w(0)
+        regroup_w(2, nc.vector.tensor_copy)
+        quantise_w(1)
+        quantise_w(2)
+        swap_sin(0, TAB)
+
+        products = {}
+        sums = {}
+        factors = {}
+
+        def take_factors(t):
+            factor = small.tile([P, 3 * H], F32, name="factor")
+            nc.scalar.activation(
+                out=factor[:], in_=sums[t][:], func=ACT.Abs_reciprocal_sqrt, bias=eps_tile[:, 0:1], scale=1.0 / HD
+            )
+            factors[t] = factor
+
+        def finish(t):
+            chunk, in_chunk = divmod(t, TAB)
+            y = products[t]
+            factor = factors[t]
+            pair = pair_behind_tile.get(t)
+            if pair is not None and pair % 2 == 1 and t > 0:
+                copy_x(pair, x_copier(pair))
+            if t % 2 == 0 and t >= 2 and t // 2 + 1 < NPAIR:
+                quantise_x(t // 2 + 1)
+            both = work.tile([P, 2, 2, H * HD], F32, name="both")
+            for k in range(2):
+                for h in range(H):
+                    nc.vector.scalar_tensor_tensor(
+                        out=both[:, k, :, h * HD : (h + 1) * HD],
+                        in0=y[k][:, h : h + 1, :].to_broadcast([P, 2, HD]),
+                        scalar=factor[:, k * H + h : k * H + h + 1],
+                        in1=table[:, t, k, :, :],
+                        op0=ALU.mult,
+                        op1=ALU.mult,
+                    )
+            v_out = work.tile([P, H, HD], F32, name="v_out")
+            nc.vector.tensor_tensor(
+                out=v_out[:],
+                in0=y[2][:],
+                in1=factor[:, 2 * H : 3 * H].unsqueeze(2).to_broadcast([P, H, HD]),
+                op=ALU.mult,
+            )
+            if in_chunk < 2 and chunk + 2 < NTAB:
+                build_table(chunk + 2, in_chunk)
+            qk_out = work.tile([P, 2, H * HD], F32, name="qk_out")
+            out_halves = qk_out[:].rearrange("p k (m s i) -> p k m s i", s=2, i=16)
+            halves = both[:].rearrange("p k two (m s i) -> p k two m s i", s=2, i=16)
+            adder = nc.vector if t == NT - 1 else nc.gpsimd
+            for s in range(2):
+                adder.tensor_tensor(
+                    out=out_halves[:, :, :, s, :],
+                    in0=halves[:, :, 0, :, s, :],
+                    in1=halves[:, :, 1, :, 1 - s, :],
+                    op=ALU.add,
+                )
+            nc.sync.dma_start(out=out_views[2][:, t, :], in_=v_out[:].rearrange("p h f -> p (h f)"))
+            nc.sync.dma_start(out=out_views[0][:, t, :], in_=qk_out[:, 0, :])
+            nc.sync.dma_start(out=out_views[1][:, t, :], in_=qk_out[:, 1, :])
+
+        for t in range(NT):
+            codes, scales = x_codes[t // 2]
+            tokens = slice((t % 2) * P, (t % 2 + 1) * P)
+            y = []
+            for i in range(3):
+                bank = psum_y.tile([P, H, HD], F32, name="y_bank")
+                nc.tensor.matmul_mx(
+                    out=bank[:].rearrange("p h f -> p (h f)"),
+                    lhsT=codes[:, tokens].bitcast(FP8X4),
+                    lhsT_scale=scales[:, tokens],
+                    rhs=w_codes[:, i * D : (i + 1) * D].bitcast(FP8X4),
+                    rhs_scale=w_scales[:, i * D : (i + 1) * D],
+                    start=True,
+                    stop=True,
+                )
+                y.append(bank)
+            products[t] = y
+            pair = pair_behind_tile.get(t)
+            if pair is not None:
+                transpose_x(pair)
+            if t == 0:
+                copy_x(1, x_copier(1))
+                swap_sin(TAB, NT)
+                quantise_x(1)
+                for chunk in range(2):
+                    for product in range(2):
+                        build_table(chunk, product)
+
+            squares = small.tile([P, 3 * H], F32, name="squares")
+            sums[t] = squares
+            for j in range(3 * H):
+                unused = small.tile([P, HD], BF16, name="unused")
+                nc.scalar.activation(
+                    out=unused[:], in_=y[j // H][:, j % H, :], func=ACT.Square, accum_out=squares[:, j : j + 1]
+                )
+                if j == LAG - 1 and t > 0:
+                    take_factors(t - 1)
+            if pair is not None and pair % 2 == 0:
+                copy_x(pair, x_copier(pair))
+            if t > 0:
+                finish(t - 1)
+        take_factors(NT - 1)
+        finish(NT - 1)

@@ -18,6 +18,7 @@ NT = N // P
 NPAIR = NT // 2
 TAB = 4
 NTAB = NT // TAB
+V_SCALAR = 4
 LAG = 4
 RING = 7
 EPS = 1e-6
@@ -35,6 +36,7 @@ def tile_torchgemma4visionattention_pa_t_kernel(
         x_grouped = ctx.enter_context(tc.tile_pool(name="x_grouped", bufs=2))
         x_mx = ctx.enter_context(tc.tile_pool(name="x_mx", bufs=4))
         small = ctx.enter_context(tc.tile_pool(name="small", bufs=4))
+        spill = ctx.enter_context(tc.tile_pool(name="spill", bufs=3 * H))
         work = ctx.enter_context(tc.tile_pool(name="work", bufs=4))
         psum_t = ctx.enter_context(tc.psum_pool(name="psum_t", bufs=1))
         psum_y = ctx.enter_context(tc.psum_pool(name="psum_y", bufs=RING))
@@ -148,7 +150,7 @@ def tile_torchgemma4visionattention_pa_t_kernel(
         def x_copier(pair):
             return nc.scalar.copy if pair % 2 == 0 else nc.vector.tensor_copy
 
-        pair_behind_tile = {max(2 * pair - 3, 0): pair for pair in range(1, NPAIR)}
+        pair_behind_tile = {max(2 * pair - 4, pair - 1): pair for pair in range(1, NPAIR)}
 
         transpose_x(0)
         copy_x(0, x_copier(0))
@@ -177,10 +179,6 @@ def tile_torchgemma4visionattention_pa_t_kernel(
             y = products[t]
             factor = factors[t]
             pair = pair_behind_tile.get(t)
-            if pair is not None and pair % 2 == 1 and t > 0:
-                copy_x(pair, x_copier(pair))
-            if t % 2 == 0 and t >= 2 and t // 2 + 1 < NPAIR:
-                quantise_x(t // 2 + 1)
             both = work.tile([P, 2, 2, H * HD], F32, name="both")
             for k in range(2):
                 for h in range(H):
@@ -192,15 +190,19 @@ def tile_torchgemma4visionattention_pa_t_kernel(
                         op0=ALU.mult,
                         op1=ALU.mult,
                     )
-            v_out = work.tile([P, H, HD], F32, name="v_out")
+            if pair is not None and pair % 2 == 1 and t > 0:
+                copy_x(pair, x_copier(pair))
+            if t % 2 == 1 and (t + 3) // 2 < NPAIR:
+                quantise_x((t + 3) // 2)
+            v_out = v_outs[t]
             nc.vector.tensor_tensor(
-                out=v_out[:],
-                in0=y[2][:],
-                in1=factor[:, 2 * H : 3 * H].unsqueeze(2).to_broadcast([P, H, HD]),
+                out=v_out[:, V_SCALAR:H, :],
+                in0=y[2][:, V_SCALAR:H, :],
+                in1=factor[:, 2 * H + V_SCALAR : 3 * H].unsqueeze(2).to_broadcast([P, H - V_SCALAR, HD]),
                 op=ALU.mult,
             )
-            if in_chunk < 2 and chunk + 2 < NTAB:
-                build_table(chunk + 2, in_chunk)
+            if in_chunk % 2 == 0 and chunk + 2 < NTAB:
+                build_table(chunk + 2, in_chunk // 2)
             qk_out = work.tile([P, 2, H * HD], F32, name="qk_out")
             out_halves = qk_out[:].rearrange("p k (m s i) -> p k m s i", s=2, i=16)
             halves = both[:].rearrange("p k two (m s i) -> p k two m s i", s=2, i=16)
@@ -215,6 +217,19 @@ def tile_torchgemma4visionattention_pa_t_kernel(
             nc.sync.dma_start(out=out_views[2][:, t, :], in_=v_out[:].rearrange("p h f -> p (h f)"))
             nc.sync.dma_start(out=out_views[0][:, t, :], in_=qk_out[:, 0, :])
             nc.sync.dma_start(out=out_views[1][:, t, :], in_=qk_out[:, 1, :])
+
+        v_outs = {}
+
+        def scale_v(t):
+            v_out = work.tile([P, H, HD], F32, name="v_out")
+            for h in range(V_SCALAR):
+                nc.scalar.activation(
+                    out=v_out[:, h, :],
+                    in_=products[t][2][:, h, :],
+                    func=ACT.Copy,
+                    scale=factors[t][:, 2 * H + h : 2 * H + h + 1],
+                )
+            v_outs[t] = v_out
 
         for t in range(NT):
             codes, scales = x_codes[t // 2]
@@ -247,15 +262,18 @@ def tile_torchgemma4visionattention_pa_t_kernel(
             squares = small.tile([P, 3 * H], F32, name="squares")
             sums[t] = squares
             for j in range(3 * H):
-                unused = small.tile([P, HD], BF16, name="unused")
+                unused = spill.tile([P, HD], BF16, name="unused")
                 nc.scalar.activation(
                     out=unused[:], in_=y[j // H][:, j % H, :], func=ACT.Square, accum_out=squares[:, j : j + 1]
                 )
                 if j == LAG - 1 and t > 0:
                     take_factors(t - 1)
+                if j == 2 * LAG - 1 and t > 0:
+                    scale_v(t - 1)
             if pair is not None and pair % 2 == 0:
                 copy_x(pair, x_copier(pair))
             if t > 0:
                 finish(t - 1)
         take_factors(NT - 1)
+        scale_v(NT - 1)
         finish(NT - 1)

@@ -16,9 +16,10 @@ P = 128
 PACK = 4
 NT = N // P
 NPAIR = NT // 2
-TAB = 4
+TAB = 2
+FIRST = 2 * TAB
 NTAB = NT // TAB
-V_SCALAR = 4
+V_SCALAR = 3
 LAG = 4
 RING = 7
 EPS = 1e-6
@@ -59,20 +60,24 @@ def tile_torchgemma4visionattention_pa_t_kernel(
             nc.sync.dma_start(out=raw[:], in_=x_view[:, 2 * pair : 2 * pair + 2, :])
             x_raw.append(raw)
 
-        gains = const.tile([P, 2, HD], BF16, name="gains")
+        gain_row = const.tile([P, 2 * HD], BF16, name="gain_row")
+        ones = const.tile([P, P], BF16, name="ones")
+        nc.vector.memset(gain_row[:], 0.0)
+        nc.vector.memset(ones[:], 1.0)
+        nc.scalar.dma_start(out=gain_row[0:1, 0:HD], in_=q_scale.unsqueeze(0))
+        nc.scalar.dma_start(out=gain_row[0:1, HD : 2 * HD], in_=k_scale.unsqueeze(0))
+        gains = const.tile([P, 2, HD], F32, name="gains")
         cos_sb = const.tile([P, NT, HD], BF16, name="cos_sb")
         sin_sb = const.tile([P, NT, HD], BF16, name="sin_sb")
         load_x(0)
         load_w(Wq, "q")
+        nc.sync.dma_start(out=sin_sb[:, 0:FIRST, :], in_=sin_view[:, 0:FIRST, :])
+        nc.sync.dma_start(out=cos_sb[:, 0:FIRST, :], in_=cos_view[:, 0:FIRST, :])
         load_w(Wk, "k")
         load_w(Wv, "v")
-        nc.sync.dma_start(out=gains[:, 0, :], in_=q_scale.partition_broadcast(P))
-        nc.sync.dma_start(out=gains[:, 1, :], in_=k_scale.partition_broadcast(P))
-        nc.sync.dma_start(out=cos_sb[:, 0:TAB, :], in_=cos_view[:, 0:TAB, :])
-        nc.sync.dma_start(out=sin_sb[:, 0:TAB, :], in_=sin_view[:, 0:TAB, :])
         load_x(1)
-        nc.sync.dma_start(out=sin_sb[:, TAB:NT, :], in_=sin_view[:, TAB:NT, :])
-        nc.sync.dma_start(out=cos_sb[:, TAB:NT, :], in_=cos_view[:, TAB:NT, :])
+        nc.sync.dma_start(out=sin_sb[:, FIRST:NT, :], in_=sin_view[:, FIRST:NT, :])
+        nc.sync.dma_start(out=cos_sb[:, FIRST:NT, :], in_=cos_view[:, FIRST:NT, :])
         for pair in range(2, NPAIR):
             load_x(pair)
 
@@ -103,13 +108,18 @@ def tile_torchgemma4visionattention_pa_t_kernel(
         sin_swapped = const.tile([P, NT, HD], BF16, name="sin_swapped")
         table = const.tile([P, NT, 2, 2, HD], F32, name="table")
 
-        def swap_sin(t0, t1):
+        def swap_sin(t0, t1, engine):
             plain = sin_sb[:, t0:t1, :].rearrange("p t (b s i) -> p (t b) s i", b=2, s=2)
             swapped = sin_swapped[:, t0:t1, :].rearrange("p t (b s i) -> p (t b) s i", b=2, s=2)
-            nc.vector.tensor_copy(out=swapped[:, :, 0, :], in_=plain[:, :, 1, :])
-            nc.vector.tensor_scalar(
-                out=swapped[:, :, 1, :], in0=plain[:, :, 0, :], scalar1=-1.0, scalar2=None, op0=ALU.mult
-            )
+            for s, sign in ((0, 1.0), (1, -1.0)):
+                engine.tensor_scalar(
+                    out=swapped[:, :, s, :],
+                    in0=plain[:, :, 1 - s, :],
+                    scalar1=sign,
+                    scalar2=1.0,
+                    op0=ALU.mult,
+                    op1=ALU.mult,
+                )
 
         def build_table(chunk, product):
             tiles = slice(chunk * TAB, (chunk + 1) * TAB)
@@ -150,29 +160,40 @@ def tile_torchgemma4visionattention_pa_t_kernel(
         def x_copier(pair):
             return nc.scalar.copy if pair % 2 == 0 else nc.vector.tensor_copy
 
-        pair_behind_tile = {max(2 * pair - 4, pair - 1): pair for pair in range(1, NPAIR)}
+        pair_behind_tile = {max(2 * pair - 4, 1): pair for pair in range(2, NPAIR)}
 
         transpose_x(0)
+        gain_bank = psum_y.tile([P, H, HD], F32, name="y_bank")
+        nc.tensor.matmul(
+            gain_bank[:, 0:2, :].rearrange("p k f -> p (k f)"), lhsT=ones[:], rhs=gain_row[:], start=True, stop=True
+        )
         copy_x(0, x_copier(0))
+        nc.scalar.copy(out=gains[:], in_=gain_bank[:, 0:2, :])
         regroup_w(0, nc.vector.tensor_copy)
         regroup_w(1, nc.scalar.copy)
         quantise_x(0)
+        swap_sin(0, FIRST, nc.vector)
         quantise_w(0)
         regroup_w(2, nc.vector.tensor_copy)
         quantise_w(1)
         quantise_w(2)
-        swap_sin(0, TAB)
+        for chunk in range(2):
+            for product in range(2):
+                build_table(chunk, product)
+        swap_sin(FIRST, NT, nc.gpsimd)
 
         products = {}
         sums = {}
         factors = {}
 
-        def take_factors(t):
-            factor = small.tile([P, 3 * H], F32, name="factor")
+        def take_factors(t, heads):
             nc.scalar.activation(
-                out=factor[:], in_=sums[t][:], func=ACT.Abs_reciprocal_sqrt, bias=eps_tile[:, 0:1], scale=1.0 / HD
+                out=factors[t][:, heads],
+                in_=sums[t][:, heads],
+                func=ACT.Abs_reciprocal_sqrt,
+                bias=eps_tile[:, 0:1],
+                scale=1.0 / HD,
             )
-            factors[t] = factor
 
         def finish(t):
             chunk, in_chunk = divmod(t, TAB)
@@ -190,39 +211,47 @@ def tile_torchgemma4visionattention_pa_t_kernel(
                         op0=ALU.mult,
                         op1=ALU.mult,
                     )
-            if pair is not None and pair % 2 == 1 and t > 0:
-                copy_x(pair, x_copier(pair))
+                if k == 0 and pair is not None and pair % 2 == 1:
+                    copy_x(pair, x_copier(pair))
+            if t == 0:
+                quantise_x(1)
             if t % 2 == 1 and (t + 3) // 2 < NPAIR:
                 quantise_x((t + 3) // 2)
             v_out = v_outs[t]
-            nc.vector.tensor_tensor(
-                out=v_out[:, V_SCALAR:H, :],
-                in0=y[2][:, V_SCALAR:H, :],
-                in1=factor[:, 2 * H + V_SCALAR : 3 * H].unsqueeze(2).to_broadcast([P, H - V_SCALAR, HD]),
-                op=ALU.mult,
-            )
-            if in_chunk % 2 == 0 and chunk + 2 < NTAB:
-                build_table(chunk + 2, in_chunk // 2)
+            n = v_heads(t)
+            if n < H:
+                nc.vector.tensor_tensor(
+                    out=v_out[:, n:H, :],
+                    in0=y[2][:, n:H, :],
+                    in1=factor[:, 2 * H + n : 3 * H].unsqueeze(2).to_broadcast([P, H - n, HD]),
+                    op=ALU.mult,
+                )
+            if chunk + 2 < NTAB:
+                build_table(chunk + 2, in_chunk)
             qk_out = work.tile([P, 2, H * HD], F32, name="qk_out")
             out_halves = qk_out[:].rearrange("p k (m s i) -> p k m s i", s=2, i=16)
             halves = both[:].rearrange("p k two (m s i) -> p k two m s i", s=2, i=16)
-            adder = nc.vector if t == NT - 1 else nc.gpsimd
-            for s in range(2):
-                adder.tensor_tensor(
-                    out=out_halves[:, :, :, s, :],
-                    in0=halves[:, :, 0, :, s, :],
-                    in1=halves[:, :, 1, :, 1 - s, :],
-                    op=ALU.add,
-                )
+            shares = [(slice(0, 2), nc.gpsimd)] if t < NT - 1 else [(slice(0, 1), nc.gpsimd), (slice(1, 2), nc.vector)]
+            for share, adder in shares:
+                for s in range(2):
+                    adder.tensor_tensor(
+                        out=out_halves[:, share, :, s, :],
+                        in0=halves[:, share, 0, :, s, :],
+                        in1=halves[:, share, 1, :, 1 - s, :],
+                        op=ALU.add,
+                    )
             nc.sync.dma_start(out=out_views[2][:, t, :], in_=v_out[:].rearrange("p h f -> p (h f)"))
             nc.sync.dma_start(out=out_views[0][:, t, :], in_=qk_out[:, 0, :])
             nc.sync.dma_start(out=out_views[1][:, t, :], in_=qk_out[:, 1, :])
 
         v_outs = {}
 
+        def v_heads(t):
+            return V_SCALAR if t < NT - 1 else H
+
         def scale_v(t):
             v_out = work.tile([P, H, HD], F32, name="v_out")
-            for h in range(V_SCALAR):
+            for h in range(v_heads(t)):
                 nc.scalar.activation(
                     out=v_out[:, h, :],
                     in_=products[t][2][:, h, :],
@@ -247,33 +276,33 @@ def tile_torchgemma4visionattention_pa_t_kernel(
                     stop=True,
                 )
                 y.append(bank)
+                if t == 0 and i == 0:
+                    transpose_x(1)
+                    copy_x(1, nc.vector.tensor_copy)
             products[t] = y
             pair = pair_behind_tile.get(t)
             if pair is not None:
                 transpose_x(pair)
-            if t == 0:
-                copy_x(1, x_copier(1))
-                swap_sin(TAB, NT)
-                quantise_x(1)
-                for chunk in range(2):
-                    for product in range(2):
-                        build_table(chunk, product)
-
             squares = small.tile([P, 3 * H], F32, name="squares")
             sums[t] = squares
+            factors[t] = small.tile([P, 3 * H], F32, name="factor")
+            by_projection = t in (0, NT - 1)
             for j in range(3 * H):
                 unused = spill.tile([P, HD], BF16, name="unused")
                 nc.scalar.activation(
                     out=unused[:], in_=y[j // H][:, j % H, :], func=ACT.Square, accum_out=squares[:, j : j + 1]
                 )
+                i, h = divmod(j, H)
+                if h == LAG - 1 and i > 0 and by_projection:
+                    take_factors(t, slice((i - 1) * H, i * H))
                 if j == LAG - 1 and t > 0:
-                    take_factors(t - 1)
+                    take_factors(t - 1, slice(2 * H, 3 * H) if t == 1 else slice(0, 3 * H))
                 if j == 2 * LAG - 1 and t > 0:
                     scale_v(t - 1)
             if pair is not None and pair % 2 == 0:
                 copy_x(pair, x_copier(pair))
             if t > 0:
                 finish(t - 1)
-        take_factors(NT - 1)
+        take_factors(NT - 1, slice(2 * H, 3 * H))
         scale_v(NT - 1)
         finish(NT - 1)

@@ -16,8 +16,7 @@ P = 128
 PACK = 4
 NT = N // P
 NPAIR = NT // 2
-TAB = 2
-FIRST = 2 * TAB
+TAB = 4
 NTAB = NT // TAB
 V_SCALAR = 3
 LAG = 4
@@ -66,18 +65,18 @@ def tile_torchgemma4visionattention_pa_t_kernel(
         nc.vector.memset(ones[:], 1.0)
         nc.scalar.dma_start(out=gain_row[0:1, 0:HD], in_=q_scale.unsqueeze(0))
         nc.scalar.dma_start(out=gain_row[0:1, HD : 2 * HD], in_=k_scale.unsqueeze(0))
-        gains = const.tile([P, 2, HD], F32, name="gains")
+        gains = const.tile([P, 2, HD], BF16, name="gains")
         cos_sb = const.tile([P, NT, HD], BF16, name="cos_sb")
         sin_sb = const.tile([P, NT, HD], BF16, name="sin_sb")
         load_x(0)
         load_w(Wq, "q")
-        nc.sync.dma_start(out=sin_sb[:, 0:FIRST, :], in_=sin_view[:, 0:FIRST, :])
-        nc.sync.dma_start(out=cos_sb[:, 0:FIRST, :], in_=cos_view[:, 0:FIRST, :])
+        nc.sync.dma_start(out=sin_sb[:, 0:TAB, :], in_=sin_view[:, 0:TAB, :])
+        nc.sync.dma_start(out=cos_sb[:, 0:TAB, :], in_=cos_view[:, 0:TAB, :])
         load_w(Wk, "k")
         load_w(Wv, "v")
         load_x(1)
-        nc.sync.dma_start(out=sin_sb[:, FIRST:NT, :], in_=sin_view[:, FIRST:NT, :])
-        nc.sync.dma_start(out=cos_sb[:, FIRST:NT, :], in_=cos_view[:, FIRST:NT, :])
+        nc.sync.dma_start(out=sin_sb[:, TAB:NT, :], in_=sin_view[:, TAB:NT, :])
+        nc.sync.dma_start(out=cos_sb[:, TAB:NT, :], in_=cos_view[:, TAB:NT, :])
         for pair in range(2, NPAIR):
             load_x(pair)
 
@@ -108,18 +107,13 @@ def tile_torchgemma4visionattention_pa_t_kernel(
         sin_swapped = const.tile([P, NT, HD], BF16, name="sin_swapped")
         table = const.tile([P, NT, 2, 2, HD], F32, name="table")
 
-        def swap_sin(t0, t1, engine):
+        def swap_sin(t0, t1):
             plain = sin_sb[:, t0:t1, :].rearrange("p t (b s i) -> p (t b) s i", b=2, s=2)
             swapped = sin_swapped[:, t0:t1, :].rearrange("p t (b s i) -> p (t b) s i", b=2, s=2)
-            for s, sign in ((0, 1.0), (1, -1.0)):
-                engine.tensor_scalar(
-                    out=swapped[:, :, s, :],
-                    in0=plain[:, :, 1 - s, :],
-                    scalar1=sign,
-                    scalar2=1.0,
-                    op0=ALU.mult,
-                    op1=ALU.mult,
-                )
+            nc.vector.tensor_copy(out=swapped[:, :, 0, :], in_=plain[:, :, 1, :])
+            nc.vector.tensor_scalar(
+                out=swapped[:, :, 1, :], in0=plain[:, :, 0, :], scalar1=-1.0, scalar2=None, op0=ALU.mult
+            )
 
         def build_table(chunk, product):
             tiles = slice(chunk * TAB, (chunk + 1) * TAB)
@@ -172,15 +166,13 @@ def tile_torchgemma4visionattention_pa_t_kernel(
         regroup_w(0, nc.vector.tensor_copy)
         regroup_w(1, nc.scalar.copy)
         quantise_x(0)
-        swap_sin(0, FIRST, nc.vector)
+        swap_sin(0, TAB)
         quantise_w(0)
         regroup_w(2, nc.vector.tensor_copy)
         quantise_w(1)
         quantise_w(2)
-        for chunk in range(2):
-            for product in range(2):
-                build_table(chunk, product)
-        swap_sin(FIRST, NT, nc.gpsimd)
+        for product in range(2):
+            build_table(0, product)
 
         products = {}
         sums = {}
@@ -215,6 +207,7 @@ def tile_torchgemma4visionattention_pa_t_kernel(
                     copy_x(pair, x_copier(pair))
             if t == 0:
                 quantise_x(1)
+                swap_sin(TAB, NT)
             if t % 2 == 1 and (t + 3) // 2 < NPAIR:
                 quantise_x((t + 3) // 2)
             v_out = v_outs[t]
@@ -226,8 +219,8 @@ def tile_torchgemma4visionattention_pa_t_kernel(
                     in1=factor[:, 2 * H + n : 3 * H].unsqueeze(2).to_broadcast([P, H - n, HD]),
                     op=ALU.mult,
                 )
-            if chunk + 2 < NTAB:
-                build_table(chunk + 2, in_chunk)
+            if in_chunk % 2 == 0 and chunk + 2 < NTAB:
+                build_table(chunk + 2, in_chunk // 2)
             qk_out = work.tile([P, 2, H * HD], F32, name="qk_out")
             out_halves = qk_out[:].rearrange("p k (m s i) -> p k m s i", s=2, i=16)
             halves = both[:].rearrange("p k two (m s i) -> p k two m s i", s=2, i=16)
@@ -243,6 +236,9 @@ def tile_torchgemma4visionattention_pa_t_kernel(
             nc.sync.dma_start(out=out_views[2][:, t, :], in_=v_out[:].rearrange("p h f -> p (h f)"))
             nc.sync.dma_start(out=out_views[0][:, t, :], in_=qk_out[:, 0, :])
             nc.sync.dma_start(out=out_views[1][:, t, :], in_=qk_out[:, 1, :])
+            if t == 0:
+                for product in range(2):
+                    build_table(1, product)
 
         v_outs = {}
 

@@ -18,7 +18,6 @@ NT = N // P
 NPAIR = NT // 2
 TAB = 4
 NTAB = NT // TAB
-V_SCALAR = 3
 LAG = 4
 RING = 7
 EPS = 1e-6
@@ -38,6 +37,7 @@ def tile_torchgemma4visionattention_pa_t_kernel(
         small = ctx.enter_context(tc.tile_pool(name="small", bufs=4))
         spill = ctx.enter_context(tc.tile_pool(name="spill", bufs=3 * H))
         work = ctx.enter_context(tc.tile_pool(name="work", bufs=4))
+        chunks = ctx.enter_context(tc.tile_pool(name="chunks", bufs=2))
         psum_t = ctx.enter_context(tc.psum_pool(name="psum_t", bufs=1))
         psum_y = ctx.enter_context(tc.psum_pool(name="psum_y", bufs=RING))
 
@@ -151,9 +151,6 @@ def tile_torchgemma4visionattention_pa_t_kernel(
             )
             x_codes[pair] = (codes, scales)
 
-        def x_copier(pair):
-            return nc.scalar.copy if pair % 2 == 0 else nc.vector.tensor_copy
-
         pair_behind_tile = {max(2 * pair - 4, 1): pair for pair in range(2, NPAIR)}
 
         transpose_x(0)
@@ -161,7 +158,7 @@ def tile_torchgemma4visionattention_pa_t_kernel(
         nc.tensor.matmul(
             gain_bank[:, 0:2, :].rearrange("p k f -> p (k f)"), lhsT=ones[:], rhs=gain_row[:], start=True, stop=True
         )
-        copy_x(0, x_copier(0))
+        copy_x(0, nc.scalar.copy)
         nc.scalar.copy(out=gains[:], in_=gain_bank[:, 0:2, :])
         regroup_w(0, nc.vector.tensor_copy)
         regroup_w(1, nc.scalar.copy)
@@ -177,6 +174,9 @@ def tile_torchgemma4visionattention_pa_t_kernel(
         products = {}
         sums = {}
         factors = {}
+        boths = {}
+        qk_outs = {}
+        v_outs = {}
 
         def take_factors(t, heads):
             nc.scalar.activation(
@@ -191,8 +191,11 @@ def tile_torchgemma4visionattention_pa_t_kernel(
             chunk, in_chunk = divmod(t, TAB)
             y = products[t]
             factor = factors[t]
-            pair = pair_behind_tile.get(t)
-            both = work.tile([P, 2, 2, H * HD], F32, name="both")
+            if in_chunk == 0:
+                boths[chunk] = chunks.tile([P, TAB, 2, 2, H * HD], F32, name="both")
+                qk_outs[chunk] = chunks.tile([P, 2, TAB, H * HD], F32, name="qk_out")
+            both = boths[chunk][:, in_chunk]
+            qk_out = qk_outs[chunk]
             for k in range(2):
                 for h in range(H):
                     nc.vector.scalar_tensor_tensor(
@@ -203,27 +206,23 @@ def tile_torchgemma4visionattention_pa_t_kernel(
                         op0=ALU.mult,
                         op1=ALU.mult,
                     )
-                if k == 0 and pair is not None and pair % 2 == 1:
-                    copy_x(pair, x_copier(pair))
             if t == 0:
                 quantise_x(1)
                 swap_sin(TAB, NT)
             if t % 2 == 1 and (t + 3) // 2 < NPAIR:
                 quantise_x((t + 3) // 2)
-            v_out = v_outs[t]
-            n = v_heads(t)
-            if n < H:
+            if not v_by_scalar(t):
+                v_outs[t] = work.tile([P, H, HD], F32, name="v_out")
                 nc.vector.tensor_tensor(
-                    out=v_out[:, n:H, :],
-                    in0=y[2][:, n:H, :],
-                    in1=factor[:, 2 * H + n : 3 * H].unsqueeze(2).to_broadcast([P, H - n, HD]),
+                    out=v_outs[t][:],
+                    in0=y[2][:],
+                    in1=factor[:, 2 * H : 3 * H].unsqueeze(2).to_broadcast([P, H, HD]),
                     op=ALU.mult,
                 )
             if in_chunk % 2 == 0 and chunk + 2 < NTAB:
                 build_table(chunk + 2, in_chunk // 2)
-            qk_out = work.tile([P, 2, H * HD], F32, name="qk_out")
-            out_halves = qk_out[:].rearrange("p k (m s i) -> p k m s i", s=2, i=16)
-            halves = both[:].rearrange("p k two (m s i) -> p k two m s i", s=2, i=16)
+            out_halves = qk_out[:, :, in_chunk, :].rearrange("p k (m s i) -> p k m s i", s=2, i=16)
+            halves = both.rearrange("p k two (m s i) -> p k two m s i", s=2, i=16)
             shares = [(slice(0, 2), nc.gpsimd)] if t < NT - 1 else [(slice(0, 1), nc.gpsimd), (slice(1, 2), nc.vector)]
             for share, adder in shares:
                 for s in range(2):
@@ -233,21 +232,24 @@ def tile_torchgemma4visionattention_pa_t_kernel(
                         in1=halves[:, share, 1, :, 1 - s, :],
                         op=ALU.add,
                     )
-            nc.sync.dma_start(out=out_views[2][:, t, :], in_=v_out[:].rearrange("p h f -> p (h f)"))
-            nc.sync.dma_start(out=out_views[0][:, t, :], in_=qk_out[:, 0, :])
-            nc.sync.dma_start(out=out_views[1][:, t, :], in_=qk_out[:, 1, :])
+            nc.sync.dma_start(out=out_views[2][:, t, :], in_=v_outs[t][:].rearrange("p h f -> p (h f)"))
+            if chunk == NTAB - 1:
+                for k in range(2):
+                    nc.sync.dma_start(out=out_views[k][:, t, :], in_=qk_out[:, k, in_chunk, :])
+            elif in_chunk == TAB - 1:
+                for k in range(2):
+                    nc.sync.dma_start(out=out_views[k][:, t - TAB + 1 : t + 1, :], in_=qk_out[:, k])
             if t == 0:
                 for product in range(2):
                     build_table(1, product)
 
-        v_outs = {}
 
-        def v_heads(t):
-            return V_SCALAR if t < NT - 1 else H
+        def v_by_scalar(t):
+            return t % 5 == 0 or t == NT - 1
 
         def scale_v(t):
             v_out = work.tile([P, H, HD], F32, name="v_out")
-            for h in range(v_heads(t)):
+            for h in range(H):
                 nc.scalar.activation(
                     out=v_out[:, h, :],
                     in_=products[t][2][:, h, :],
@@ -293,10 +295,10 @@ def tile_torchgemma4visionattention_pa_t_kernel(
                     take_factors(t, slice((i - 1) * H, i * H))
                 if j == LAG - 1 and t > 0:
                     take_factors(t - 1, slice(2 * H, 3 * H) if t == 1 else slice(0, 3 * H))
-                if j == 2 * LAG - 1 and t > 0:
+                if j == 2 * LAG - 1 and t > 0 and v_by_scalar(t - 1):
                     scale_v(t - 1)
-            if pair is not None and pair % 2 == 0:
-                copy_x(pair, x_copier(pair))
+            if pair is not None:
+                copy_x(pair, nc.scalar.copy)
             if t > 0:
                 finish(t - 1)
         take_factors(NT - 1, slice(2 * H, 3 * H))

@@ -17,6 +17,7 @@ PACK = 4
 NT = N // P
 NPAIR = NT // 2
 TAB = 4
+FIRST = 2 * TAB
 NTAB = NT // TAB
 LAG = 4
 RING = 7
@@ -70,13 +71,13 @@ def tile_torchgemma4visionattention_pa_t_kernel(
         sin_sb = const.tile([P, NT, HD], BF16, name="sin_sb")
         load_x(0)
         load_w(Wq, "q")
-        nc.sync.dma_start(out=sin_sb[:, 0:TAB, :], in_=sin_view[:, 0:TAB, :])
-        nc.sync.dma_start(out=cos_sb[:, 0:TAB, :], in_=cos_view[:, 0:TAB, :])
+        nc.sync.dma_start(out=sin_sb[:, 0:FIRST, :], in_=sin_view[:, 0:FIRST, :])
+        nc.sync.dma_start(out=cos_sb[:, 0:FIRST, :], in_=cos_view[:, 0:FIRST, :])
         load_w(Wk, "k")
         load_w(Wv, "v")
         load_x(1)
-        nc.sync.dma_start(out=sin_sb[:, TAB:NT, :], in_=sin_view[:, TAB:NT, :])
-        nc.sync.dma_start(out=cos_sb[:, TAB:NT, :], in_=cos_view[:, TAB:NT, :])
+        nc.sync.dma_start(out=sin_sb[:, FIRST:NT, :], in_=sin_view[:, FIRST:NT, :])
+        nc.sync.dma_start(out=cos_sb[:, FIRST:NT, :], in_=cos_view[:, FIRST:NT, :])
         for pair in range(2, NPAIR):
             load_x(pair)
 
@@ -159,17 +160,18 @@ def tile_torchgemma4visionattention_pa_t_kernel(
             gain_bank[:, 0:2, :].rearrange("p k f -> p (k f)"), lhsT=ones[:], rhs=gain_row[:], start=True, stop=True
         )
         copy_x(0, nc.scalar.copy)
-        nc.scalar.copy(out=gains[:], in_=gain_bank[:, 0:2, :])
         regroup_w(0, nc.vector.tensor_copy)
         regroup_w(1, nc.scalar.copy)
         quantise_x(0)
-        swap_sin(0, TAB)
+        swap_sin(0, FIRST)
         quantise_w(0)
+        nc.vector.tensor_copy(out=gains[:], in_=gain_bank[:, 0:2, :])
         regroup_w(2, nc.vector.tensor_copy)
         quantise_w(1)
         quantise_w(2)
-        for product in range(2):
-            build_table(0, product)
+        for chunk in range(2):
+            for product in range(2):
+                build_table(chunk, product)
 
         products = {}
         sums = {}
@@ -193,13 +195,13 @@ def tile_torchgemma4visionattention_pa_t_kernel(
             factor = factors[t]
             if in_chunk == 0:
                 boths[chunk] = chunks.tile([P, TAB, 2, 2, H * HD], F32, name="both")
-                qk_outs[chunk] = chunks.tile([P, 2, TAB, H * HD], F32, name="qk_out")
+                qk_outs[chunk] = chunks.tile([P, TAB, 2, H * HD], F32, name="qk_out")
             both = boths[chunk][:, in_chunk]
-            qk_out = qk_outs[chunk]
+            qk_out = qk_outs[chunk][:, in_chunk]
             for k in range(2):
                 for h in range(H):
                     nc.vector.scalar_tensor_tensor(
-                        out=both[:, k, :, h * HD : (h + 1) * HD],
+                        out=both[:, :, k, h * HD : (h + 1) * HD],
                         in0=y[k][:, h : h + 1, :].to_broadcast([P, 2, HD]),
                         scalar=factor[:, k * H + h : k * H + h + 1],
                         in1=table[:, t, k, :, :],
@@ -208,7 +210,7 @@ def tile_torchgemma4visionattention_pa_t_kernel(
                     )
             if t == 0:
                 quantise_x(1)
-                swap_sin(TAB, NT)
+                swap_sin(FIRST, NT)
             if t % 2 == 1 and (t + 3) // 2 < NPAIR:
                 quantise_x((t + 3) // 2)
             if not v_by_scalar(t):
@@ -221,27 +223,20 @@ def tile_torchgemma4visionattention_pa_t_kernel(
                 )
             if in_chunk % 2 == 0 and chunk + 2 < NTAB:
                 build_table(chunk + 2, in_chunk // 2)
-            out_halves = qk_out[:, :, in_chunk, :].rearrange("p k (m s i) -> p k m s i", s=2, i=16)
-            halves = both.rearrange("p k two (m s i) -> p k two m s i", s=2, i=16)
-            shares = [(slice(0, 2), nc.gpsimd)] if t < NT - 1 else [(slice(0, 1), nc.gpsimd), (slice(1, 2), nc.vector)]
+            shares = [(slice(0, 2), nc.gpsimd)] if t < NT - 1 else [(slice(k, k + 1), nc.vector) for k in range(2)]
             for share, adder in shares:
-                for s in range(2):
-                    adder.tensor_tensor(
-                        out=out_halves[:, share, :, s, :],
-                        in0=halves[:, share, 0, :, s, :],
-                        in1=halves[:, share, 1, :, 1 - s, :],
-                        op=ALU.add,
-                    )
+                first, second, total = [
+                    a.rearrange("p k (m s i) -> p (k m) s i", s=2, i=16)
+                    for a in (both[:, 0, share], both[:, 1, share], qk_out[:, share])
+                ]
+                adder.tensor_tensor(out=total, in0=first, in1=second[:, :, ::-1, :], op=ALU.add)
             nc.sync.dma_start(out=out_views[2][:, t, :], in_=v_outs[t][:].rearrange("p h f -> p (h f)"))
             if chunk == NTAB - 1:
                 for k in range(2):
-                    nc.sync.dma_start(out=out_views[k][:, t, :], in_=qk_out[:, k, in_chunk, :])
+                    nc.sync.dma_start(out=out_views[k][:, t, :], in_=qk_out[:, k, :])
             elif in_chunk == TAB - 1:
                 for k in range(2):
-                    nc.sync.dma_start(out=out_views[k][:, t - TAB + 1 : t + 1, :], in_=qk_out[:, k])
-            if t == 0:
-                for product in range(2):
-                    build_table(1, product)
+                    nc.sync.dma_start(out=out_views[k][:, t - TAB + 1 : t + 1, :], in_=qk_outs[chunk][:, :, k, :])
 
 
         def v_by_scalar(t):

from contextlib import ExitStack

import concourse.mybir as mybir
from concourse.masks import make_identity

F32 = mybir.dt.float32
BF16 = mybir.dt.bfloat16
U32 = mybir.dt.uint32
U8 = mybir.dt.uint8
FP8X4 = mybir.dt.float8_e4m3fn_x4
ALU = mybir.AluOpType
ACT = mybir.ActivationFunctionType

N, D, H, HD = 4096, 512, 8, 64
P = 128
PACK = 4
NT = N // P
NPAIR = NT // 2
TAB = 4
FIRST = 2 * TAB
NTAB = NT // TAB
LAG = 4
RING = 7
EPS = 1e-6
FLOPS = 2 * N * D * 3 * H * HD


def tile_torchgemma4visionattention_pa_t_kernel(
    tc, hidden_states, cos, sin, Wq, Wk, Wv, q_scale, k_scale, out_0, out_1, out_2
):
    nc = tc.nc
    with ExitStack() as ctx:
        ctx.enter_context(tc.manual_schedule())
        const = ctx.enter_context(tc.tile_pool(name="const", bufs=1))
        x_in = ctx.enter_context(tc.tile_pool(name="x_in", bufs=NPAIR))
        x_grouped = ctx.enter_context(tc.tile_pool(name="x_grouped", bufs=2))
        x_mx = ctx.enter_context(tc.tile_pool(name="x_mx", bufs=4))
        small = ctx.enter_context(tc.tile_pool(name="small", bufs=4))
        spill = ctx.enter_context(tc.tile_pool(name="spill", bufs=3 * H))
        work = ctx.enter_context(tc.tile_pool(name="work", bufs=4))
        chunks = ctx.enter_context(tc.tile_pool(name="chunks", bufs=2))
        psum_t = ctx.enter_context(tc.psum_pool(name="psum_t", bufs=1))
        psum_y = ctx.enter_context(tc.psum_pool(name="psum_y", bufs=RING))

        x_view = hidden_states.rearrange("(p t) d -> p t d", t=NT)
        cos_view = cos.rearrange("(p t) f -> p t f", t=NT)
        sin_view = sin.rearrange("(p t) f -> p t f", t=NT)
        out_views = [o.rearrange("(p t) h f -> p t (h f)", t=NT) for o in (out_0, out_1, out_2)]

        w_raw = []
        x_raw = []

        def load_w(w, label):
            raw = const.tile([P, PACK, D], BF16, name="w_raw_" + label)
            nc.sync.dma_start(out=raw[:], in_=w.rearrange("(p j) c -> p j c", j=PACK))
            w_raw.append(raw)

        def load_x(pair):
            raw = x_in.tile([P, 2, D], BF16, name="x_raw")
            nc.sync.dma_start(out=raw[:], in_=x_view[:, 2 * pair : 2 * pair + 2, :])
            x_raw.append(raw)

        gain_row = const.tile([P, 2 * HD], BF16, name="gain_row")
        ones = const.tile([P, P], BF16, name="ones")
        nc.vector.memset(gain_row[:], 0.0)
        nc.vector.memset(ones[:], 1.0)
        nc.scalar.dma_start(out=gain_row[0:1, 0:HD], in_=q_scale.unsqueeze(0))
        nc.scalar.dma_start(out=gain_row[0:1, HD : 2 * HD], in_=k_scale.unsqueeze(0))
        gains = const.tile([P, 2, HD], BF16, name="gains")
        cos_sb = const.tile([P, NT, HD], BF16, name="cos_sb")
        sin_sb = const.tile([P, NT, HD], BF16, name="sin_sb")
        load_x(0)
        load_w(Wq, "q")
        nc.sync.dma_start(out=sin_sb[:, 0:FIRST, :], in_=sin_view[:, 0:FIRST, :])
        nc.sync.dma_start(out=cos_sb[:, 0:FIRST, :], in_=cos_view[:, 0:FIRST, :])
        load_w(Wk, "k")
        load_w(Wv, "v")
        load_x(1)
        nc.sync.dma_start(out=sin_sb[:, FIRST:NT, :], in_=sin_view[:, FIRST:NT, :])
        nc.sync.dma_start(out=cos_sb[:, FIRST:NT, :], in_=cos_view[:, FIRST:NT, :])
        for pair in range(2, NPAIR):
            load_x(pair)

        identity = const.tile([P, P], F32, name="identity")
        make_identity(nc, identity[:])
        eps_tile = const.tile([P, 1], F32, name="eps_tile")
        nc.vector.memset(eps_tile[:], EPS)
        warm = const.tile([P, 1], F32, name="warm")
        nc.scalar.activation(out=warm[:], in_=eps_tile[:], func=ACT.Abs_reciprocal_sqrt)

        w_codes = const.tile([P, 3 * D], U32, name="w_codes", align_bytes=64)
        w_scales = const.tile([P, 3 * D], U8, name="w_scales", align_bytes=64)
        w_grouped = [const.tile([P, D, PACK], BF16, name="w_grouped%d" % i, align_bytes=64) for i in range(3)]

        def regroup_w(i, copy):
            copy(
                out=w_grouped[i][:].rearrange("p (c i) t -> p c t i", i=4),
                in_=w_raw[i][:].rearrange("p t (c i) -> p c t i", i=4),
            )

        def quantise_w(i):
            nc.vector.quantize_mx(
                out=w_codes[:, i * D : (i + 1) * D].bitcast(FP8X4),
                scales=w_scales[:, i * D : (i + 1) * D],
                in_=w_grouped[i][:].rearrange("p c t -> p (c t)"),
            )

        sin_swapped = const.tile([P, NT, HD], BF16, name="sin_swapped")
        table = const.tile([P, NT, 2, 2, HD], F32, name="table")

        def swap_sin(t0, t1):
            plain = sin_sb[:, t0:t1, :].rearrange("p t (b s i) -> p (t b) s i", b=2, s=2)
            swapped = sin_swapped[:, t0:t1, :].rearrange("p t (b s i) -> p (t b) s i", b=2, s=2)
            nc.vector.tensor_copy(out=swapped[:, :, 0, :], in_=plain[:, :, 1, :])
            nc.vector.tensor_scalar(
                out=swapped[:, :, 1, :], in0=plain[:, :, 0, :], scalar1=-1.0, scalar2=None, op0=ALU.mult
            )

        def build_table(chunk, product):
            tiles = slice(chunk * TAB, (chunk + 1) * TAB)
            angle = cos_sb if product == 0 else sin_swapped
            nc.gpsimd.tensor_tensor(
                out=table[:, tiles, :, product, :],
                in0=angle[:, tiles, :].unsqueeze(2).to_broadcast([P, TAB, 2, HD]),
                in1=gains[:].unsqueeze(1).to_broadcast([P, TAB, 2, HD]),
                op=ALU.mult,
            )

        x_banks = {}
        x_groups = {}
        x_codes = {}

        def transpose_x(pair):
            words = x_raw[pair][:].bitcast(F32)
            bank = psum_t.tile([P, 2, 2, P], F32, name="x_bank")
            for a in range(2):
                for u in range(2):
                    nc.tensor.transpose(bank[:, a, u, :], words[:, a, u : 2 * P : 2], identity[:])
            x_banks[pair] = bank

        def copy_x(pair, copy):
            grouped = x_grouped.tile([P, 2, P, PACK], BF16, name="x_group", align_bytes=64)
            as_words = grouped[:].rearrange("p a n t -> p a (n t)").bitcast(F32).rearrange("p a (n u) -> p a n u", u=2)
            copy(out=as_words, in_=x_banks[pair][:].rearrange("p a u n -> p a n u"))
            x_groups[pair] = grouped

        def quantise_x(pair):
            codes = x_mx.tile([P, 2 * P], U32, name="x_code", align_bytes=64)
            scales = x_mx.tile([P, 2 * P], U8, name="x_scale", align_bytes=64)
            nc.vector.quantize_mx(
                out=codes[:].bitcast(FP8X4), scales=scales[:], in_=x_groups[pair][:].rearrange("p a n t -> p (a n t)")
            )
            x_codes[pair] = (codes, scales)

        pair_behind_tile = {max(2 * pair - 4, 1): pair for pair in range(2, NPAIR)}

        transpose_x(0)
        gain_bank = psum_y.tile([P, H, HD], F32, name="y_bank")
        nc.tensor.matmul(
            gain_bank[:, 0:2, :].rearrange("p k f -> p (k f)"), lhsT=ones[:], rhs=gain_row[:], start=True, stop=True
        )
        copy_x(0, nc.scalar.copy)
        regroup_w(0, nc.vector.tensor_copy)
        regroup_w(1, nc.scalar.copy)
        quantise_x(0)
        swap_sin(0, FIRST)
        quantise_w(0)
        nc.vector.tensor_copy(out=gains[:], in_=gain_bank[:, 0:2, :])
        regroup_w(2, nc.vector.tensor_copy)
        quantise_w(1)
        quantise_w(2)
        for chunk in range(2):
            for product in range(2):
                build_table(chunk, product)

        products = {}
        sums = {}
        factors = {}
        boths = {}
        qk_outs = {}
        v_outs = {}

        def take_factors(t, heads):
            nc.scalar.activation(
                out=factors[t][:, heads],
                in_=sums[t][:, heads],
                func=ACT.Abs_reciprocal_sqrt,
                bias=eps_tile[:, 0:1],
                scale=1.0 / HD,
            )

        def finish(t):
            chunk, in_chunk = divmod(t, TAB)
            y = products[t]
            factor = factors[t]
            if in_chunk == 0:
                boths[chunk] = chunks.tile([P, TAB, 2, 2, H * HD], F32, name="both")
                qk_outs[chunk] = chunks.tile([P, TAB, 2, H * HD], F32, name="qk_out")
            both = boths[chunk][:, in_chunk]
            qk_out = qk_outs[chunk][:, in_chunk]
            for k in range(2):
                for h in range(H):
                    nc.vector.scalar_tensor_tensor(
                        out=both[:, :, k, h * HD : (h + 1) * HD],
                        in0=y[k][:, h : h + 1, :].to_broadcast([P, 2, HD]),
                        scalar=factor[:, k * H + h : k * H + h + 1],
                        in1=table[:, t, k, :, :],
                        op0=ALU.mult,
                        op1=ALU.mult,
                    )
            if t == 0:
                quantise_x(1)
                swap_sin(FIRST, NT)
            if t % 2 == 1 and (t + 3) // 2 < NPAIR:
                quantise_x((t + 3) // 2)
            if not v_by_scalar(t):
                v_outs[t] = work.tile([P, H, HD], F32, name="v_out")
                nc.vector.tensor_tensor(
                    out=v_outs[t][:],
                    in0=y[2][:],
                    in1=factor[:, 2 * H : 3 * H].unsqueeze(2).to_broadcast([P, H, HD]),
                    op=ALU.mult,
                )
            if in_chunk % 2 == 0 and chunk + 2 < NTAB:
                build_table(chunk + 2, in_chunk // 2)
            shares = [(slice(0, 2), nc.gpsimd)] if t < NT - 1 else [(slice(k, k + 1), nc.vector) for k in range(2)]
            for share, adder in shares:
                first, second, total = [
                    a.rearrange("p k (m s i) -> p (k m) s i", s=2, i=16)
                    for a in (both[:, 0, share], both[:, 1, share], qk_out[:, share])
                ]
                adder.tensor_tensor(out=total, in0=first, in1=second[:, :, ::-1, :], op=ALU.add)
            nc.sync.dma_start(out=out_views[2][:, t, :], in_=v_outs[t][:].rearrange("p h f -> p (h f)"))
            if chunk == NTAB - 1:
                for k in range(2):
                    nc.sync.dma_start(out=out_views[k][:, t, :], in_=qk_out[:, k, :])
            elif in_chunk == TAB - 1:
                for k in range(2):
                    nc.sync.dma_start(out=out_views[k][:, t - TAB + 1 : t + 1, :], in_=qk_outs[chunk][:, :, k, :])


        def v_by_scalar(t):
            return t % 5 == 0 or t == NT - 1

        def scale_v(t):
            v_out = work.tile([P, H, HD], F32, name="v_out")
            for h in range(H):
                nc.scalar.activation(
                    out=v_out[:, h, :],
                    in_=products[t][2][:, h, :],
                    func=ACT.Copy,
                    scale=factors[t][:, 2 * H + h : 2 * H + h + 1],
                )
            v_outs[t] = v_out

        for t in range(NT):
            codes, scales = x_codes[t // 2]
            tokens = slice((t % 2) * P, (t % 2 + 1) * P)
            y = []
            for i in range(3):
                bank = psum_y.tile([P, H, HD], F32, name="y_bank")
                nc.tensor.matmul_mx(
                    out=bank[:].rearrange("p h f -> p (h f)"),
                    lhsT=codes[:, tokens].bitcast(FP8X4),
                    lhsT_scale=scales[:, tokens],
                    rhs=w_codes[:, i * D : (i + 1) * D].bitcast(FP8X4),
                    rhs_scale=w_scales[:, i * D : (i + 1) * D],
                    start=True,
                    stop=True,
                )
                y.append(bank)
                if t == 0 and i == 0:
                    transpose_x(1)
                    copy_x(1, nc.vector.tensor_copy)
            products[t] = y
            pair = pair_behind_tile.get(t)
            if pair is not None:
                transpose_x(pair)
            squares = small.tile([P, 3 * H], F32, name="squares")
            sums[t] = squares
            factors[t] = small.tile([P, 3 * H], F32, name="factor")
            by_projection = t in (0, NT - 1)
            for j in range(3 * H):
                unused = spill.tile([P, HD], BF16, name="unused")
                nc.scalar.activation(
                    out=unused[:], in_=y[j // H][:, j % H, :], func=ACT.Square, accum_out=squares[:, j : j + 1]
                )
                i, h = divmod(j, H)
                if h == LAG - 1 and i > 0 and by_projection:
                    take_factors(t, slice((i - 1) * H, i * H))
                if j == LAG - 1 and t > 0:
                    take_factors(t - 1, slice(2 * H, 3 * H) if t == 1 else slice(0, 3 * H))
                if j == 2 * LAG - 1 and t > 0 and v_by_scalar(t - 1):
                    scale_v(t - 1)
            if pair is not None:
                copy_x(pair, nc.scalar.copy)
            if t > 0:
                finish(t - 1)
        take_factors(NT - 1, slice(2 * H, 3 * H))
        scale_v(NT - 1)
        finish(NT - 1)
